import numpy as np
import ml_dtypes


def mxq(x, axis, fmt="e4m3"):
    dtype, down = {"e4m3": (ml_dtypes.float8_e4m3fn, 7), "e5m2": (ml_dtypes.float8_e5m2, 14)}[fmt]
    v = np.moveaxis(np.asarray(x, np.float32).astype(ml_dtypes.bfloat16).astype(np.float64), axis, -1)
    blocks = v.reshape(v.shape[:-1] + (-1, 32))
    amax = np.abs(blocks).max(-1, keepdims=True)
    byte = np.maximum(np.where(amax > 0, np.frexp(amax)[1] - 1 + 127, 0) - down, 1)
    scale = np.exp2(byte - 127.0)
    codes = (blocks / scale).astype(np.float32).astype(dtype).astype(np.float64)
    return np.moveaxis((codes * scale).reshape(v.shape), -1, axis)


WIDE = False


def mx_kscale(k):
    if not WIDE:
        return np.ones(k)
    levels = np.array([10, -10, 5, -5, 0])
    a = np.random.permutation(np.resize(levels, k // 512 * 4)).reshape(k // 512, 4)
    idx = np.arange(k)
    return np.exp2(a[idx // 512, idx % 128 // 32])


BF16 = ml_dtypes.bfloat16


def bf(x):
    return np.asarray(x, np.float32).astype(BF16)


def f64(x):
    return np.asarray(x).astype(np.float64)


E2M1 = np.array([0.0, 0.5, 1.0, 1.5, 2.0, 3.0, 4.0, 6.0, -0.0, -0.5, -1.0, -1.5, -2.0, -3.0, -4.0, -6.0])


def pack_weight(w, fmt):
    k, n = w.shape
    w = f64(bf(w)).reshape(k // 32, 32, n)
    amax = np.abs(w).max(1)
    if fmt == "e4m3":
        byte = np.frexp(amax)[1] - 1 + 127 - 7
    else:
        mant, ex = np.frexp(amax / 6.0)
        byte = np.where(mant > 0.5, ex, ex - 1) + 127
    byte = np.clip(np.where(amax > 0, byte, 1), 1, 254)
    scaled = (w * np.exp2(127.0 - byte)[:, None, :]).reshape(k, n).astype(np.float32)
    by_word = np.ascontiguousarray(scaled.reshape(k // 512, 128, 4, n).transpose(0, 1, 3, 2))
    if fmt == "e4m3":
        words = by_word.astype(ml_dtypes.float8_e4m3fn).view(np.uint8)
    else:
        c = by_word.astype(ml_dtypes.float4_e2m1fn).view(np.uint8) & 0xF
        words = c[..., 0::2] | (c[..., 1::2] << 4)
    return np.ascontiguousarray(words), np.ascontiguousarray(byte.astype(np.uint8).reshape(k // 512, 16, n))


def unpack_weight(words, scales, fmt):
    g, p, n, _ = words.shape
    if fmt == "e4m3":
        vals = np.ascontiguousarray(words).view(ml_dtypes.float8_e4m3fn).astype(np.float64)
    else:
        nib = np.empty((g, p, n, 4), np.uint8)
        nib[..., 0::2] = words & 0xF
        nib[..., 1::2] = words >> 4
        vals = E2M1[nib]
    vals = vals * np.repeat(np.exp2(scales.astype(np.float64) - 127.0), 8, axis=1)[..., None]
    return vals.transpose(0, 1, 3, 2).reshape(g * 512, n)


B, IN_F, OUT_F = 64, 8192, 8192
IN_Q = IN_F // 4
OUT_Q = OUT_F // 4
FMT = "e4m3"


def setup_inputs():
    s = mx_kscale(IN_Q)
    scale = 1.0 / np.sqrt(IN_Q)
    inp = {"x": bf((np.random.standard_normal((B, 4, IN_Q)) * s).reshape(B, IN_F))}
    for name in ["rr", "ri", "rj", "rk"]:
        w = np.random.uniform(-scale, scale, (OUT_Q, IN_Q)) / s[None, :]
        words, scales = pack_weight(np.ascontiguousarray(w.T), FMT)
        inp["W_" + name + "_words"] = words
        inp["W_" + name + "_scales"] = scales
    for name in ["rr", "ri", "rj", "rk"]:
        inp["b_" + name] = bf(np.random.standard_normal(OUT_Q) * 0.5)
    return inp


def reference(x, W_rr_words, W_rr_scales, W_ri_words, W_ri_scales, W_rj_words, W_rj_scales, W_rk_words, W_rk_scales, b_rr, b_ri, b_rj, b_rk):
    b = x.shape[0]
    xs = f64(x).reshape(b, 4, IN_Q)
    bias = np.stack([f64(b_rr), f64(b_ri), f64(b_rj), f64(b_rk)])
    xq = mxq(xs, 2, "e4m3")
    Wq = np.stack([
        unpack_weight(W_rr_words, W_rr_scales, FMT).T,
        unpack_weight(W_ri_words, W_ri_scales, FMT).T,
        unpack_weight(W_rj_words, W_rj_scales, FMT).T,
        unpack_weight(W_rk_words, W_rk_scales, FMT).T,
    ])
    Y = (xq.reshape(b * 4, IN_Q) @ Wq.reshape(4 * OUT_Q, IN_Q).T).reshape(b, 4, 4, OUT_Q) + bias
    out_r = Y[:, 0, 0] - Y[:, 1, 1] - Y[:, 2, 2] - Y[:, 3, 3]
    out_i = Y[:, 0, 1] + Y[:, 1, 0] + Y[:, 2, 3] - Y[:, 3, 2]
    out_j = Y[:, 0, 2] - Y[:, 1, 3] + Y[:, 2, 0] + Y[:, 3, 1]
    out_k = Y[:, 0, 3] + Y[:, 1, 2] - Y[:, 2, 1] + Y[:, 3, 0]
    out = np.stack([out_r, out_i, out_j, out_k], axis=1)
    return out.reshape(b, -1)

@@ -1,0 +1,212 @@
+from contextlib import ExitStack
+
+import concourse.mybir as mybir
+from concourse.masks import make_identity
+
+F32 = mybir.dt.float32
+BF16 = mybir.dt.bfloat16
+I32 = mybir.dt.int32
+U32 = mybir.dt.uint32
+U8 = mybir.dt.uint8
+FP8X4 = mybir.dt.float8_e4m3fn_x4
+ADD = mybir.AluOpType.add
+
+FLOPS = 2 * 256 * 8192 * 2048
+
+P = 128
+NQ = 4
+NG = 4
+NT = 512
+
+VARIANTS = (
+    ((1, 0, -1.0), (1, 1, 1.0)),
+    ((0, 0, 1.0), (0, 1, -1.0)),
+    ((0, 1, -1.0), (0, 0, 1.0)),
+    ((1, 1, -1.0), (1, 0, 1.0)),
+    ((1, 1, -1.0), (1, 0, -1.0)),
+    ((0, 1, 1.0), (0, 0, 1.0)),
+)
+NEGATIVE_BIAS = ((1, 0, 0), (2, 0, 0), (3, 0, 0), (3, 0, 1), (2, 1, 0), (1, 1, 1))
+
+
+def tile_qdense_w_kernel(
+    tc,
+    x,
+    W_rr_words,
+    W_rr_scales,
+    W_ri_words,
+    W_ri_scales,
+    W_rj_words,
+    W_rj_scales,
+    W_rk_words,
+    W_rk_scales,
+    b_rr,
+    b_ri,
+    b_rj,
+    b_rk,
+    out,
+):
+    nc = tc.nc
+    w_words = (W_rr_words, W_ri_words, W_rj_words, W_rk_words)
+    w_scales = (W_rr_scales, W_ri_scales, W_rj_scales, W_rk_scales)
+    biases = (b_rr, b_ri, b_rj, b_rk)
+
+    with ExitStack() as ctx:
+        keep = ctx.enter_context(tc.tile_pool(name="keep", bufs=1))
+        stage = ctx.enter_context(tc.tile_pool(name="stage", bufs=3))
+        psum = ctx.enter_context(tc.psum_pool(name="psum", bufs=1))
+
+        ww = {}
+        for q in range(NQ):
+            for g in range(NG):
+                ww[(q, g)] = keep.tile([P, 2048], U32, name="ww%d%d" % (q, g), align_bytes=64)
+        wp = [keep.tile([P, 2048], U8, name="wp%d" % q, align_bytes=64) for q in range(NQ)]
+        x_sb = keep.tile([P, NG, 2, 512], BF16, name="x_sb", align_bytes=64)
+        grp = keep.tile([P, NG, 2, P, 4], BF16, name="grp", align_bytes=64)
+        xwn = keep.tile([P, NG, 2, P], U32, name="xwn", align_bytes=64)
+        xpn = keep.tile([P, NG, 2, P], U8, name="xpn", align_bytes=64)
+        xwv = keep.tile([P, 6, NG, P], U32, name="xwv", align_bytes=64)
+        xpv = keep.tile([P, 6, NG, P], U8, name="xpv", align_bytes=64)
+        ident = keep.tile([P, P], F32, name="ident")
+        brow = keep.tile([P, 2048], BF16, name="brow")
+        sgn = keep.tile([P, 2, P], BF16, name="sgn")
+        res = keep.tile([P, 4096], F32, name="res")
+
+        for q in range(NQ):
+            nc.vector.memset(wp[q][:].bitcast(I32), 0)
+        nc.vector.memset(brow[:], 0.0)
+        nc.vector.memset(sgn[:], 1.0)
+        sgn4 = sgn[:].rearrange("p t (b h) -> p t b h", h=2)
+        for q, t, h in NEGATIVE_BIAS:
+            nc.vector.memset(sgn4[32 * q : 32 * q + 32, t, :, h], -1.0)
+        make_identity(nc, ident[:])
+
+        def load_scales(q):
+            for quad in range(4):
+                nc.sync.dma_start(
+                    out=wp[q][32 * quad : 32 * quad + 16, :].bitcast(I32),
+                    in_=w_scales[q][:, 4 * quad : 4 * quad + 4, :].bitcast(I32),
+                )
+
+        def load_words(q, g, c0, c1):
+            src = w_words[q][g].rearrange("p n t -> p (n t)")[:, 4 * c0 : 4 * c1]
+            nc.sync.dma_start(out=ww[(q, g)][:, c0:c1].bitcast(I32), in_=src.bitcast(I32))
+
+        xv = x.rearrange("b (h l g c) -> (b h) l g c", h=2, l=2, g=NG)
+        for g in range(NG):
+            nc.sync.dma_start(out=x_sb[:, g, :, :], in_=xv[:, :, g, :])
+        for q in range(NQ):
+            nc.gpsimd.dma_start(
+                out=brow[32 * q : 32 * q + 1, :], in_=biases[q].rearrange("(o n) -> o n", o=1)
+            )
+        for q in range(NQ):
+            load_scales(q)
+            for g in range(NG):
+                load_words(q, g, 0, 1024)
+        for q in range(NQ - 1):
+            for g in range(NG):
+                load_words(q, g, 1024, 2048)
+        for j in (2, 3):
+            for g in range(NG):
+                load_words(NQ - 1, g, NT * j, NT * j + NT)
+
+        for g in range(NG):
+            tps = psum.tile([P, 2, 2, P], F32, name="tps%d" % g, tag="bank%d" % (4 + g))
+            for l in range(2):
+                words = x_sb[:, g, l, :].bitcast(F32)
+                for u in range(2):
+                    nc.tensor.transpose(tps[:, l, u, :], words[:, u:256:2], ident[:])
+            nc.scalar.copy(
+                out=grp[:, g, :, :, :].bitcast(F32), in_=tps[:].rearrange("p l u m -> p l m u")
+            )
+            nc.vector.quantize_mx(
+                out=xwn[:, g, :, :].rearrange("p l m -> p (l m)").bitcast(FP8X4),
+                scales=xpn[:, g, :, :].rearrange("p l m -> p (l m)"),
+                in_=grp[:, g, :, :, :].rearrange("p l m t -> p (l m t)"),
+            )
+
+        grp6 = grp[:].rearrange("p g l (b h) t -> p g l b h t", h=2)
+        for v in range(6):
+            var = stage.tile([P, NG, 64, 2, 4], BF16, name="var%d" % v, tag="var", align_bytes=64)
+            for h in range(2):
+                l, hs, sign = VARIANTS[v][h]
+                dst = var[:, :, :, h, :]
+                src = grp6[:, :, l, :, hs, :]
+                if v % 2 == 0:
+                    if sign > 0:
+                        nc.vector.tensor_copy(out=dst, in_=src)
+                    else:
+                        nc.vector.tensor_scalar_mul(out=dst, in0=src, scalar1=-1.0)
+                else:
+                    if sign > 0:
+                        nc.scalar.copy(out=dst, in_=src)
+                    else:
+                        nc.scalar.mul(out=dst, in_=src, mul=-1.0)
+            nc.vector.quantize_mx(
+                out=xwv[:, v, :, :].rearrange("p g m -> p (g m)").bitcast(FP8X4),
+                scales=xpv[:, v, :, :].rearrange("p g m -> p (g m)"),
+                in_=var[:].rearrange("p g b h t -> p (g b h t)"),
+            )
+
+        def mx_pass(acc, t, q, g, j):
+            if q == 0:
+                lw = xwn[:, g, t, :]
+                lp = xpn[:, g, t, :]
+            else:
+                lw = xwv[:, 2 * (q - 1) + t, g, :]
+                lp = xpv[:, 2 * (q - 1) + t, g, :]
+            nc.tensor.matmul_mx(
+                out=acc[:],
+                lhsT=lw.bitcast(FP8X4),
+                lhsT_scale=lp,
+                rhs=ww[(q, g)][:, NT * j : NT * j + NT].bitcast(FP8X4),
+                rhs_scale=wp[q][4 * g : P, NT * j : NT * j + NT],
+                start=(q == 0 and g == 0),
+                stop=(q == NQ - 1 and g == NG - 1),
+            )
+
+        def bias_tile(t, j, bank):
+            bp = psum.tile([P, NT], F32, name="bp%d%d" % (t, j), tag="bank%d" % bank)
+            nc.tensor.matmul(
+                out=bp[:], lhsT=sgn[:, t, :], rhs=brow[:, NT * j : NT * j + NT], start=True, stop=True
+            )
+            nc.scalar.copy(out=res[:, 2048 * t + NT * j : 2048 * t + NT * j + NT], in_=bp[:])
+
+        out_v = out.rearrange("b (h f) -> (b h) f", h=2)
+
+        def finish(acc, t, j, queue):
+            cols = slice(2048 * t + NT * j, 2048 * t + NT * j + NT)
+            nc.vector.tensor_tensor(out=res[:, cols], in0=acc[:], in1=res[:, cols], op=ADD)
+            queue.dma_start(out=out_v[:, cols], in_=res[:, cols])
+
+        acc = {}
+        for t in range(2):
+            for j in range(2):
+                acc[(t, j)] = psum.tile([P, NT], F32, name="acc%d%d" % (t, j), tag="bank%d" % (2 * t + j))
+        for q in range(NQ):
+            for g in range(NG):
+                for t in range(2):
+                    for j in range(2):
+                        mx_pass(acc[(t, j)], t, q, g, j)
+            if q < 2:
+                for t in range(2):
+                    for j in range(2):
+                        bias_tile(t, 2 * q + j, 4 + 2 * t + j)
+        for t in range(2):
+            for j in range(2):
+                finish(acc[(t, j)], t, j, nc.scalar)
+
+        for t in range(2):
+            for j in (2, 3):
+                acc[(t, j)] = psum.tile([P, NT], F32, name="acc%d%d" % (t, j), tag="bank%d" % (2 + 2 * t + j))
+        for q in range(NQ - 1):
+            for g in range(NG):
+                for t in range(2):
+                    for j in (2, 3):
+                        mx_pass(acc[(t, j)], t, q, g, j)
+        for j in (2, 3):
+            for g in range(NG):
+                for t in range(2):
+                    mx_pass(acc[(t, j)], t, NQ - 1, g, j)
+            for t in range(2):
+                finish(acc[(t, j)], t, j, nc.sync)

@@ -53,7 +53,6 @@ def tile_qdense_w_kernel(
 
     with ExitStack() as ctx:
         keep = ctx.enter_context(tc.tile_pool(name="keep", bufs=1))
-        stage = ctx.enter_context(tc.tile_pool(name="stage", bufs=3))
         psum = ctx.enter_context(tc.psum_pool(name="psum", bufs=1))
 
         ww = {}
@@ -72,14 +71,13 @@ def tile_qdense_w_kernel(
         sgn = keep.tile([P, 2, P], BF16, name="sgn")
         res = keep.tile([P, 4096], F32, name="res")
 
-        for q in range(NQ):
-            nc.vector.memset(wp[q][:].bitcast(I32), 0)
-        nc.vector.memset(brow[:], 0.0)
-        nc.vector.memset(sgn[:], 1.0)
+        out_v = out.rearrange("b (h f) -> (b h) f", h=2)
+        xv = x.rearrange("b (h l g c) -> (b h) l g c", h=2, l=2, g=NG)
+        grp6 = grp[:].rearrange("p g l (b h) t -> p g l b h t", h=2)
         sgn4 = sgn[:].rearrange("p t (b h) -> p t b h", h=2)
-        for q, t, h in NEGATIVE_BIAS:
-            nc.vector.memset(sgn4[32 * q : 32 * q + 32, t, :, h], -1.0)
-        make_identity(nc, ident[:])
+        var = [
+            keep.tile([P, NG, 64, 2, 4], BF16, name="var%d" % v, align_bytes=64) for v in range(6)
+        ]
 
         def load_scales(q):
             for quad in range(4):
@@ -92,17 +90,92 @@ def tile_qdense_w_kernel(
             src = w_words[q][g].rearrange("p n t -> p (n t)")[:, 4 * c0 : 4 * c1]
             nc.sync.dma_start(out=ww[(q, g)][:, c0:c1].bitcast(I32), in_=src.bitcast(I32))
 
-        xv = x.rearrange("b (h l g c) -> (b h) l g c", h=2, l=2, g=NG)
-        for g in range(NG):
-            nc.sync.dma_start(out=x_sb[:, g, :, :], in_=xv[:, :, g, :])
+        def halves(v, on_vector):
+            for h in range(2):
+                l, hs, sign = VARIANTS[v][h]
+                dst = var[v][:, :, :, h, :]
+                src = grp6[:, :, l, :, hs, :]
+                if on_vector and sign > 0:
+                    nc.vector.tensor_copy(out=dst, in_=src)
+                elif on_vector:
+                    nc.vector.tensor_scalar_mul(out=dst, in0=src, scalar1=-1.0)
+                elif sign > 0:
+                    nc.scalar.copy(out=dst, in_=src)
+                else:
+                    nc.scalar.mul(out=dst, in_=src, mul=-1.0)
+
+        def quantise(v):
+            nc.vector.quantize_mx(
+                out=xwv[:, v, :, :].rearrange("p g m -> p (g m)").bitcast(FP8X4),
+                scales=xpv[:, v, :, :].rearrange("p g m -> p (g m)"),
+                in_=var[v][:].rearrange("p g b h t -> p (g b h t)"),
+            )
+
+        def mx_pass(acc, t, q, g, j):
+            if q == 0:
+                lw = xwn[:, g, t, :]
+                lp = xpn[:, g, t, :]
+            else:
+                lw = xwv[:, 2 * (q - 1) + t, g, :]
+                lp = xpv[:, 2 * (q - 1) + t, g, :]
+            nc.tensor.matmul_mx(
+                out=acc[:],
+                lhsT=lw.bitcast(FP8X4),
+                lhsT_scale=lp,
+                rhs=ww[(q, g)][:, NT * j : NT * j + NT].bitcast(FP8X4),
+                rhs_scale=wp[q][4 * g : P, NT * j : NT * j + NT],
+                start=(q == 0 and g == 0),
+                stop=(q == NQ - 1 and g == NG - 1),
+            )
+
+        def block(acc, q, js):
+            for g in range(NG):
+                for t in range(2):
+                    for j in js:
+                        mx_pass(acc[(t, j)], t, q, g, j)
+
+        def bias_round(js):
+            made = []
+            for t in range(2):
+                for j in js:
+                    bp = psum.tile([P, NT], F32, name="bp%d%d" % (t, j), tag="bank%d" % (4 + 2 * t + j % 2))
+                    nc.tensor.matmul(
+                        out=bp[:], lhsT=sgn[:, t, :], rhs=brow[:, NT * j : NT * j + NT], start=True, stop=True
+                    )
+                    made.append((bp, 2048 * t + NT * j))
+            for bp, c0 in made:
+                nc.scalar.copy(out=res[:, c0 : c0 + NT], in_=bp[:])
+
+        def add_bias(acc, t, j):
+            c0 = 2048 * t + NT * j
+            nc.vector.tensor_tensor(out=res[:, c0 : c0 + NT], in0=acc[(t, j)][:], in1=res[:, c0 : c0 + NT], op=ADD)
+
+        def store(c0, c1):
+            nc.sync.dma_start(out=out_v[:, c0:c1], in_=res[:, c0:c1])
+
+        ctx.enter_context(tc.manual_schedule())
+
+        nc.vector.memset(wp[0][:].bitcast(I32), 0)
+        nc.vector.memset(brow[:], 0.0)
+        for q in range(1, NQ):
+            nc.vector.memset(wp[q][:].bitcast(I32), 0)
+        nc.vector.memset(sgn[:], 1.0)
+        for q, t, h in NEGATIVE_BIAS:
+            nc.vector.memset(sgn4[32 * q : 32 * q + 32, t, :, h], -1.0)
+        make_identity(nc, ident[:])
         for q in range(NQ):
             nc.gpsimd.dma_start(
                 out=brow[32 * q : 32 * q + 1, :], in_=biases[q].rearrange("(o n) -> o n", o=1)
             )
+
+        for g in range(NG):
+            nc.sync.dma_start(out=x_sb[:, g, :, :], in_=xv[:, :, g, :])
+        load_scales(0)
         for q in range(NQ):
-            load_scales(q)
             for g in range(NG):
                 load_words(q, g, 0, 1024)
+                if g == 1 and q < NQ - 1:
+                    load_scales(q + 1)
         for q in range(NQ - 1):
             for g in range(NG):
                 load_words(q, g, 1024, 2048)
@@ -124,89 +197,42 @@ def tile_qdense_w_kernel(
                 scales=xpn[:, g, :, :].rearrange("p l m -> p (l m)"),
                 in_=grp[:, g, :, :, :].rearrange("p l m t -> p (l m t)"),
             )
-
-        grp6 = grp[:].rearrange("p g l (b h) t -> p g l b h t", h=2)
-        for v in range(6):
-            var = stage.tile([P, NG, 64, 2, 4], BF16, name="var%d" % v, tag="var", align_bytes=64)
-            for h in range(2):
-                l, hs, sign = VARIANTS[v][h]
-                dst = var[:, :, :, h, :]
-                src = grp6[:, :, l, :, hs, :]
-                if v % 2 == 0:
-                    if sign > 0:
-                        nc.vector.tensor_copy(out=dst, in_=src)
-                    else:
-                        nc.vector.tensor_scalar_mul(out=dst, in0=src, scalar1=-1.0)
-                else:
-                    if sign > 0:
-                        nc.scalar.copy(out=dst, in_=src)
-                    else:
-                        nc.scalar.mul(out=dst, in_=src, mul=-1.0)
-            nc.vector.quantize_mx(
-                out=xwv[:, v, :, :].rearrange("p g m -> p (g m)").bitcast(FP8X4),
-                scales=xpv[:, v, :, :].rearrange("p g m -> p (g m)"),
-                in_=var[:].rearrange("p g b h t -> p (g b h t)"),
-            )
-
-        def mx_pass(acc, t, q, g, j):
-            if q == 0:
-                lw = xwn[:, g, t, :]
-                lp = xpn[:, g, t, :]
-            else:
-                lw = xwv[:, 2 * (q - 1) + t, g, :]
-                lp = xpv[:, 2 * (q - 1) + t, g, :]
-            nc.tensor.matmul_mx(
-                out=acc[:],
-                lhsT=lw.bitcast(FP8X4),
-                lhsT_scale=lp,
-                rhs=ww[(q, g)][:, NT * j : NT * j + NT].bitcast(FP8X4),
-                rhs_scale=wp[q][4 * g : P, NT * j : NT * j + NT],
-                start=(q == 0 and g == 0),
-                stop=(q == NQ - 1 and g == NG - 1),
-            )
-
-        def bias_tile(t, j, bank):
-            bp = psum.tile([P, NT], F32, name="bp%d%d" % (t, j), tag="bank%d" % bank)
-            nc.tensor.matmul(
-                out=bp[:], lhsT=sgn[:, t, :], rhs=brow[:, NT * j : NT * j + NT], start=True, stop=True
-            )
-            nc.scalar.copy(out=res[:, 2048 * t + NT * j : 2048 * t + NT * j + NT], in_=bp[:])
-
-        out_v = out.rearrange("b (h f) -> (b h) f", h=2)
-
-        def finish(acc, t, j, queue):
-            cols = slice(2048 * t + NT * j, 2048 * t + NT * j + NT)
-            nc.vector.tensor_tensor(out=res[:, cols], in0=acc[:], in1=res[:, cols], op=ADD)
-            queue.dma_start(out=out_v[:, cols], in_=res[:, cols])
+        halves(0, True)
+        halves(1, False)
+        halves(2, True)
+        quantise(0)
+        quantise(1)
+        halves(3, False)
+        halves(4, True)
+        quantise(2)
+        quantise(3)
 
         acc = {}
         for t in range(2):
             for j in range(2):
                 acc[(t, j)] = psum.tile([P, NT], F32, name="acc%d%d" % (t, j), tag="bank%d" % (2 * t + j))
-        for q in range(NQ):
-            for g in range(NG):
-                for t in range(2):
-                    for j in range(2):
-                        mx_pass(acc[(t, j)], t, q, g, j)
-            if q < 2:
-                for t in range(2):
-                    for j in range(2):
-                        bias_tile(t, 2 * q + j, 4 + 2 * t + j)
+        block(acc, 0, (0, 1))
+        bias_round((0, 1))
+        halves(5, False)
+        quantise(4)
+        quantise(5)
+        block(acc, 1, (0, 1))
+        bias_round((2, 3))
+        block(acc, 2, (0, 1))
+        block(acc, 3, (0, 1))
         for t in range(2):
             for j in range(2):
-                finish(acc[(t, j)], t, j, nc.scalar)
+                add_bias(acc, t, j)
 
         for t in range(2):
             for j in (2, 3):
                 acc[(t, j)] = psum.tile([P, NT], F32, name="acc%d%d" % (t, j), tag="bank%d" % (2 + 2 * t + j))
         for q in range(NQ - 1):
-            for g in range(NG):
-                for t in range(2):
-                    for j in (2, 3):
-                        mx_pass(acc[(t, j)], t, q, g, j)
+            block(acc, q, (2, 3))
+        store(0, 1024)
+        store(2048, 3072)
         for j in (2, 3):
-            for g in range(NG):
-                for t in range(2):
-                    mx_pass(acc[(t, j)], t, NQ - 1, g, j)
+            block(acc, NQ - 1, (j,))
             for t in range(2):
-                finish(acc[(t, j)], t, j, nc.sync)
+                add_bias(acc, t, j)
+                store(2048 * t + NT * j, 2048 * t + NT * j + NT)

@@ -81,10 +81,12 @@ def tile_qdense_w_kernel(
 
         def load_scales(q):
             for quad in range(4):
-                nc.sync.dma_start(
-                    out=wp[q][32 * quad : 32 * quad + 16, :].bitcast(I32),
-                    in_=w_scales[q][:, 4 * quad : 4 * quad + 4, :].bitcast(I32),
-                )
+                dst = wp[q][32 * quad : 32 * quad + 16, :]
+                src = w_scales[q][:, 4 * quad : 4 * quad + 4, :]
+                if q == 0:
+                    nc.sync.dma_start(out=dst.bitcast(I32), in_=src.bitcast(I32))
+                else:
+                    nc.gpsimd.dma_start(out=dst.bitcast(F32), in_=src.bitcast(F32))
 
         def load_words(q, g, c0, c1):
             src = w_words[q][g].rearrange("p n t -> p (n t)")[:, 4 * c0 : 4 * c1]
@@ -155,18 +157,19 @@ def tile_qdense_w_kernel(
 
         ctx.enter_context(tc.manual_schedule())
 
-        nc.vector.memset(wp[0][:].bitcast(I32), 0)
         nc.vector.memset(brow[:], 0.0)
-        for q in range(1, NQ):
+        for q in range(NQ):
             nc.vector.memset(wp[q][:].bitcast(I32), 0)
         nc.vector.memset(sgn[:], 1.0)
         for q, t, h in NEGATIVE_BIAS:
             nc.vector.memset(sgn4[32 * q : 32 * q + 32, t, :, h], -1.0)
         make_identity(nc, ident[:])
         for q in range(NQ):
-            nc.gpsimd.dma_start(
+            nc.scalar.dma_start(
                 out=brow[32 * q : 32 * q + 1, :], in_=biases[q].rearrange("(o n) -> o n", o=1)
             )
+        for q in range(1, NQ):
+            load_scales(q)
 
         for g in range(NG):
             nc.sync.dma_start(out=x_sb[:, g, :, :], in_=xv[:, :, g, :])
@@ -174,8 +177,6 @@ def tile_qdense_w_kernel(
         for q in range(NQ):
             for g in range(NG):
                 load_words(q, g, 0, 1024)
-                if g == 1 and q < NQ - 1:
-                    load_scales(q + 1)
         for q in range(NQ - 1):
             for g in range(NG):
                 load_words(q, g, 1024, 2048)

@@ -17,6 +17,7 @@ P = 128
 NQ = 4
 NG = 4
 NT = 512
+ALL_G = (0, 1, 2, 3)
 
 VARIANTS = (
     ((1, 0, -1.0), (1, 1, 1.0)),
@@ -60,7 +61,7 @@ def tile_qdense_w_kernel(
             for g in range(NG):
                 ww[(q, g)] = keep.tile([P, 2048], U32, name="ww%d%d" % (q, g), align_bytes=64)
         wp = [keep.tile([P, 2048], U8, name="wp%d" % q, align_bytes=64) for q in range(NQ)]
-        x_sb = keep.tile([P, NG, 2, 512], BF16, name="x_sb", align_bytes=64)
+        x_sb = keep.tile([P, 2, 2, 1024], BF16, name="x_sb", align_bytes=64)
         grp = keep.tile([P, NG, 2, P, 4], BF16, name="grp", align_bytes=64)
         xwn = keep.tile([P, NG, 2, P], U32, name="xwn", align_bytes=64)
         xpn = keep.tile([P, NG, 2, P], U8, name="xpn", align_bytes=64)
@@ -72,7 +73,7 @@ def tile_qdense_w_kernel(
         res = keep.tile([P, 4096], F32, name="res")
 
         out_v = out.rearrange("b (h f) -> (b h) f", h=2)
-        xv = x.rearrange("b (h l g c) -> (b h) l g c", h=2, l=2, g=NG)
+        xv = x.rearrange("b (h l s c) -> (b h) l s c", h=2, l=2, s=2)
         grp6 = grp[:].rearrange("p g l (b h) t -> p g l b h t", h=2)
         sgn4 = sgn[:].rearrange("p t (b h) -> p t b h", h=2)
         var = [
@@ -81,12 +82,10 @@ def tile_qdense_w_kernel(
 
         def load_scales(q):
             for quad in range(4):
-                dst = wp[q][32 * quad : 32 * quad + 16, :]
-                src = w_scales[q][:, 4 * quad : 4 * quad + 4, :]
-                if q == 0:
-                    nc.sync.dma_start(out=dst.bitcast(I32), in_=src.bitcast(I32))
-                else:
-                    nc.gpsimd.dma_start(out=dst.bitcast(F32), in_=src.bitcast(F32))
+                nc.sync.dma_start(
+                    out=wp[q][32 * quad : 32 * quad + 16, :].bitcast(I32),
+                    in_=w_scales[q][:, 4 * quad : 4 * quad + 4, :].bitcast(I32),
+                )
 
         def load_words(q, g, c0, c1):
             src = w_words[q][g].rearrange("p n t -> p (n t)")[:, 4 * c0 : 4 * c1]
@@ -130,8 +129,8 @@ def tile_qdense_w_kernel(
                 stop=(q == NQ - 1 and g == NG - 1),
             )
 
-        def block(acc, q, js):
-            for g in range(NG):
+        def block(acc, q, js, gs):
+            for g in gs:
                 for t in range(2):
                     for j in js:
                         mx_pass(acc[(t, j)], t, q, g, j)
@@ -157,39 +156,45 @@ def tile_qdense_w_kernel(
 
         ctx.enter_context(tc.manual_schedule())
 
+        nc.vector.memset(wp[0][:].bitcast(I32), 0)
         nc.vector.memset(brow[:], 0.0)
-        for q in range(NQ):
+        for q in range(1, NQ):
             nc.vector.memset(wp[q][:].bitcast(I32), 0)
         nc.vector.memset(sgn[:], 1.0)
         for q, t, h in NEGATIVE_BIAS:
             nc.vector.memset(sgn4[32 * q : 32 * q + 32, t, :, h], -1.0)
         make_identity(nc, ident[:])
-        for q in range(NQ):
-            nc.scalar.dma_start(
-                out=brow[32 * q : 32 * q + 1, :], in_=biases[q].rearrange("(o n) -> o n", o=1)
-            )
-        for q in range(1, NQ):
-            load_scales(q)
 
-        for g in range(NG):
-            nc.sync.dma_start(out=x_sb[:, g, :, :], in_=xv[:, :, g, :])
+        for s in range(2):
+            nc.sync.dma_start(out=x_sb[:, s, :, :], in_=xv[:, :, s, :])
         load_scales(0)
-        for q in range(NQ):
+        for g in range(NG):
+            load_words(0, g, 0, 1024)
+            if g == 1:
+                for q in range(NQ):
+                    nc.scalar.dma_start(
+                        out=brow[32 * q : 32 * q + 1, :], in_=biases[q].rearrange("(o n) -> o n", o=1)
+                    )
+        for g in range(NG):
+            load_words(0, g, 1024, 2048)
+            if g == 1:
+                load_scales(1)
+        for q in (1, 2):
             for g in range(NG):
-                load_words(q, g, 0, 1024)
-        for q in range(NQ - 1):
+                load_words(q, g, 0, 2048)
+                if g == 2:
+                    load_scales(q + 1)
+        for c0, c1 in ((0, 1024), (1024, 1536), (1536, 2048)):
             for g in range(NG):
-                load_words(q, g, 1024, 2048)
-        for j in (2, 3):
-            for g in range(NG):
-                load_words(NQ - 1, g, NT * j, NT * j + NT)
+                load_words(3, g, c0, c1)
 
         for g in range(NG):
             tps = psum.tile([P, 2, 2, P], F32, name="tps%d" % g, tag="bank%d" % (4 + g))
             for l in range(2):
-                words = x_sb[:, g, l, :].bitcast(F32)
+                words = x_sb[:, g // 2, l, :].bitcast(F32)
+                w0 = 256 * (g % 2)
                 for u in range(2):
-                    nc.tensor.transpose(tps[:, l, u, :], words[:, u:256:2], ident[:])
+                    nc.tensor.transpose(tps[:, l, u, :], words[:, w0 + u : w0 + 256 : 2], ident[:])
             nc.scalar.copy(
                 out=grp[:, g, :, :, :].bitcast(F32), in_=tps[:].rearrange("p l u m -> p l m u")
             )
@@ -198,42 +203,39 @@ def tile_qdense_w_kernel(
                 scales=xpn[:, g, :, :].rearrange("p l m -> p (l m)"),
                 in_=grp[:, g, :, :, :].rearrange("p l m t -> p (l m t)"),
             )
-        halves(0, True)
-        halves(1, False)
-        halves(2, True)
-        quantise(0)
-        quantise(1)
-        halves(3, False)
-        halves(4, True)
-        quantise(2)
-        quantise(3)
-
         acc = {}
         for t in range(2):
             for j in range(2):
                 acc[(t, j)] = psum.tile([P, NT], F32, name="acc%d%d" % (t, j), tag="bank%d" % (2 * t + j))
-        block(acc, 0, (0, 1))
+
+        block(acc, 0, (0, 1), (0,))
         bias_round((0, 1))
-        halves(5, False)
-        quantise(4)
-        quantise(5)
-        block(acc, 1, (0, 1))
+        block(acc, 0, (0, 1), (1, 2))
         bias_round((2, 3))
-        block(acc, 2, (0, 1))
-        block(acc, 3, (0, 1))
-        for t in range(2):
-            for j in range(2):
-                add_bias(acc, t, j)
+        block(acc, 0, (0, 1), (3,))
+        halves(0, True)
+        halves(1, True)
+        quantise(0)
+        quantise(1)
+        for v in (2, 3, 4, 5):
+            halves(v, False)
+            quantise(v)
 
         for t in range(2):
             for j in (2, 3):
                 acc[(t, j)] = psum.tile([P, NT], F32, name="acc%d%d" % (t, j), tag="bank%d" % (2 + 2 * t + j))
-        for q in range(NQ - 1):
-            block(acc, q, (2, 3))
+        block(acc, 0, (2, 3), ALL_G)
+        block(acc, 1, (0, 1, 2, 3), ALL_G)
+        block(acc, 2, (0, 1, 2, 3), ALL_G)
+
+        block(acc, 3, (0, 1), ALL_G)
+        for t in range(2):
+            for j in range(2):
+                add_bias(acc, t, j)
         store(0, 1024)
         store(2048, 3072)
         for j in (2, 3):
-            block(acc, NQ - 1, (j,))
+            block(acc, 3, (j,), ALL_G)
             for t in range(2):
                 add_bias(acc, t, j)
                 store(2048 * t + NT * j, 2048 * t + NT * j + NT)

@@ -135,17 +135,20 @@ def tile_qdense_w_kernel(
                     for j in js:
                         mx_pass(acc[(t, j)], t, q, g, j)
 
-        def bias_round(js):
+        def bias_round(js, bank0):
             made = []
             for t in range(2):
                 for j in js:
-                    bp = psum.tile([P, NT], F32, name="bp%d%d" % (t, j), tag="bank%d" % (4 + 2 * t + j % 2))
+                    bp = psum.tile([P, NT], F32, name="bp%d%d" % (t, j), tag="bank%d" % (bank0 + 2 * t + j % 2))
                     nc.tensor.matmul(
                         out=bp[:], lhsT=sgn[:, t, :], rhs=brow[:, NT * j : NT * j + NT], start=True, stop=True
                     )
                     made.append((bp, 2048 * t + NT * j))
-            for bp, c0 in made:
-                nc.scalar.copy(out=res[:, c0 : c0 + NT], in_=bp[:])
+            for i, (bp, c0) in enumerate(made):
+                if i % 2 == 0:
+                    nc.vector.tensor_copy(out=res[:, c0 : c0 + NT], in_=bp[:])
+                else:
+                    nc.scalar.copy(out=res[:, c0 : c0 + NT], in_=bp[:])
 
         def add_bias(acc, t, j):
             c0 = 2048 * t + NT * j
@@ -167,23 +170,19 @@ def tile_qdense_w_kernel(
 
         for s in range(2):
             nc.sync.dma_start(out=x_sb[:, s, :, :], in_=xv[:, :, s, :])
-        load_scales(0)
-        for g in range(NG):
-            load_words(0, g, 0, 1024)
-            if g == 1:
-                for q in range(NQ):
-                    nc.scalar.dma_start(
-                        out=brow[32 * q : 32 * q + 1, :], in_=biases[q].rearrange("(o n) -> o n", o=1)
-                    )
-        for g in range(NG):
-            load_words(0, g, 1024, 2048)
-            if g == 1:
-                load_scales(1)
+        for q in range(NQ):
+            nc.sync.dma_start(
+                out=brow[32 * q : 32 * q + 1, :], in_=biases[q].rearrange("(o n) -> o n", o=1)
+            )
+        for q in range(NQ):
+            load_scales(q)
+        load_words(0, 0, 0, 1024)
+        load_words(0, 0, 1024, 2048)
+        for g in range(1, NG):
+            load_words(0, g, 0, 2048)
         for q in (1, 2):
             for g in range(NG):
                 load_words(q, g, 0, 2048)
-                if g == 2:
-                    load_scales(q + 1)
         for c0, c1 in ((0, 1024), (1024, 1536), (1536, 2048)):
             for g in range(NG):
                 load_words(3, g, c0, c1)
@@ -203,16 +202,8 @@ def tile_qdense_w_kernel(
                 scales=xpn[:, g, :, :].rearrange("p l m -> p (l m)"),
                 in_=grp[:, g, :, :, :].rearrange("p l m t -> p (l m t)"),
             )
-        acc = {}
-        for t in range(2):
-            for j in range(2):
-                acc[(t, j)] = psum.tile([P, NT], F32, name="acc%d%d" % (t, j), tag="bank%d" % (2 * t + j))
-
-        block(acc, 0, (0, 1), (0,))
-        bias_round((0, 1))
-        block(acc, 0, (0, 1), (1, 2))
-        bias_round((2, 3))
-        block(acc, 0, (0, 1), (3,))
+        bias_round((0, 1), 0)
+        bias_round((2, 3), 4)
         halves(0, True)
         halves(1, True)
         quantise(0)
@@ -221,10 +212,15 @@ def tile_qdense_w_kernel(
             halves(v, False)
             quantise(v)
 
+        acc = {}
         for t in range(2):
-            for j in (2, 3):
-                acc[(t, j)] = psum.tile([P, NT], F32, name="acc%d%d" % (t, j), tag="bank%d" % (2 + 2 * t + j))
-        block(acc, 0, (2, 3), ALL_G)
+            for j in range(4):
+                acc[(t, j)] = psum.tile(
+                    [P, NT], F32, name="acc%d%d" % (t, j), tag="bank%d" % (4 * (j // 2) + 2 * t + j % 2)
+                )
+        block(acc, 0, (0, 1), (0,))
+        block(acc, 0, (2, 3), (0,))
+        block(acc, 0, (0, 1, 2, 3), (1, 2, 3))
         block(acc, 1, (0, 1, 2, 3), ALL_G)
         block(acc, 2, (0, 1, 2, 3), ALL_G)
 

@@ -82,10 +82,12 @@ def tile_qdense_w_kernel(
 
         def load_scales(q):
             for quad in range(4):
-                nc.sync.dma_start(
-                    out=wp[q][32 * quad : 32 * quad + 16, :].bitcast(I32),
-                    in_=w_scales[q][:, 4 * quad : 4 * quad + 4, :].bitcast(I32),
-                )
+                dst = wp[q][32 * quad : 32 * quad + 16, :]
+                src = w_scales[q][:, 4 * quad : 4 * quad + 4, :]
+                if q < 2:
+                    nc.sync.dma_start(out=dst.bitcast(I32), in_=src.bitcast(I32))
+                else:
+                    nc.gpsimd.dma_start(out=dst.bitcast(F32), in_=src.bitcast(F32))
 
         def load_words(q, g, c0, c1):
             src = w_words[q][g].rearrange("p n t -> p (n t)")[:, 4 * c0 : 4 * c1]

@@ -233,7 +233,8 @@ def tile_qdense_w_kernel(
         store(0, 1024)
         store(2048, 3072)
         for j in (2, 3):
-            block(acc, 3, (j,), ALL_G)
             for t in range(2):
+                for g in ALL_G:
+                    mx_pass(acc[(t, j)], t, 3, g, j)
                 add_bias(acc, t, j)
                 store(2048 * t + NT * j, 2048 * t + NT * j + NT)

@@ -61,7 +61,7 @@ def tile_qdense_w_kernel(
             for g in range(NG):
                 ww[(q, g)] = keep.tile([P, 2048], U32, name="ww%d%d" % (q, g), align_bytes=64)
         wp = [keep.tile([P, 2048], U8, name="wp%d" % q, align_bytes=64) for q in range(NQ)]
-        x_sb = keep.tile([P, 2, 2, 1024], BF16, name="x_sb", align_bytes=64)
+        x_sb = keep.tile([P, 2, 2048], BF16, name="x_sb", align_bytes=64)
         grp = keep.tile([P, NG, 2, P, 4], BF16, name="grp", align_bytes=64)
         xwn = keep.tile([P, NG, 2, P], U32, name="xwn", align_bytes=64)
         xpn = keep.tile([P, NG, 2, P], U8, name="xpn", align_bytes=64)
@@ -73,7 +73,7 @@ def tile_qdense_w_kernel(
         res = keep.tile([P, 4096], F32, name="res")
 
         out_v = out.rearrange("b (h f) -> (b h) f", h=2)
-        xv = x.rearrange("b (h l s c) -> (b h) l s c", h=2, l=2, s=2)
+        xv = x.rearrange("b (h l f) -> (b h) l f", h=2, l=2)
         grp6 = grp[:].rearrange("p g l (b h) t -> p g l b h t", h=2)
         sgn4 = sgn[:].rearrange("p t (b h) -> p t b h", h=2)
         var = [
@@ -170,19 +170,14 @@ def tile_qdense_w_kernel(
             nc.vector.memset(sgn4[32 * q : 32 * q + 32, t, :, h], -1.0)
         make_identity(nc, ident[:])
 
-        for s in range(2):
-            nc.sync.dma_start(out=x_sb[:, s, :, :], in_=xv[:, :, s, :])
+        nc.sync.dma_start(out=x_sb[:], in_=xv)
         for q in range(NQ):
             nc.sync.dma_start(
                 out=brow[32 * q : 32 * q + 1, :], in_=biases[q].rearrange("(o n) -> o n", o=1)
             )
         for q in range(NQ):
             load_scales(q)
-        load_words(0, 0, 0, 1024)
-        load_words(0, 0, 1024, 2048)
-        for g in range(1, NG):
-            load_words(0, g, 0, 2048)
-        for q in (1, 2):
+        for q in (0, 1, 2):
             for g in range(NG):
                 load_words(q, g, 0, 2048)
         for c0, c1 in ((0, 1024), (1024, 1536), (1536, 2048)):
@@ -192,8 +187,8 @@ def tile_qdense_w_kernel(
         for g in range(NG):
             tps = psum.tile([P, 2, 2, P], F32, name="tps%d" % g, tag="bank%d" % (4 + g))
             for l in range(2):
-                words = x_sb[:, g // 2, l, :].bitcast(F32)
-                w0 = 256 * (g % 2)
+                words = x_sb[:, l, :].bitcast(F32)
+                w0 = 256 * g
                 for u in range(2):
                     nc.tensor.transpose(tps[:, l, u, :], words[:, w0 + u : w0 + 256 : 2], ident[:])
             nc.scalar.copy(
@@ -220,9 +215,7 @@ def tile_qdense_w_kernel(
                 acc[(t, j)] = psum.tile(
                     [P, NT], F32, name="acc%d%d" % (t, j), tag="bank%d" % (4 * (j // 2) + 2 * t + j % 2)
                 )
-        block(acc, 0, (0, 1), (0,))
-        block(acc, 0, (2, 3), (0,))
-        block(acc, 0, (0, 1, 2, 3), (1, 2, 3))
+        block(acc, 0, (0, 1, 2, 3), ALL_G)
         block(acc, 1, (0, 1, 2, 3), ALL_G)
         block(acc, 2, (0, 1, 2, 3), ALL_G)
 
@@ -236,5 +229,16 @@ def tile_qdense_w_kernel(
             for t in range(2):
                 for g in ALL_G:
                     mx_pass(acc[(t, j)], t, 3, g, j)
-                add_bias(acc, t, j)
-                store(2048 * t + NT * j, 2048 * t + NT * j + NT)
+                if (t, j) == (1, 3):
+                    for c in (0, NT // 2):
+                        c0 = 2048 * t + NT * j + c
+                        nc.vector.tensor_tensor(
+                            out=res[:, c0 : c0 + NT // 2],
+                            in0=acc[(t, j)][:, c : c + NT // 2],
+                            in1=res[:, c0 : c0 + NT // 2],
+                            op=ADD,
+                        )
+                        store(c0, c0 + NT // 2)
+                else:
+                    add_bias(acc, t, j)
+                    store(2048 * t + NT * j, 2048 * t + NT * j + NT)

@@ -177,9 +177,12 @@ def tile_qdense_w_kernel(
             )
         for q in range(NQ):
             load_scales(q)
-        for q in (0, 1, 2):
+        for g in range(NG):
+            load_words(0, g, 0, 2048)
+        for q in (1, 2):
             for g in range(NG):
-                load_words(q, g, 0, 2048)
+                load_words(q, g, 0, 1024)
+                load_words(q, g, 1024, 2048)
         for c0, c1 in ((0, 1024), (1024, 1536), (1536, 2048)):
             for g in range(NG):
                 load_words(3, g, c0, c1)
@@ -216,8 +219,10 @@ def tile_qdense_w_kernel(
                     [P, NT], F32, name="acc%d%d" % (t, j), tag="bank%d" % (4 * (j // 2) + 2 * t + j % 2)
                 )
         block(acc, 0, (0, 1, 2, 3), ALL_G)
-        block(acc, 1, (0, 1, 2, 3), ALL_G)
-        block(acc, 2, (0, 1, 2, 3), ALL_G)
+        for q in (1, 2):
+            for g in ALL_G:
+                block(acc, q, (0, 1), (g,))
+                block(acc, q, (2, 3), (g,))
 
         block(acc, 3, (0, 1), ALL_G)
         for t in range(2):

@@ -161,24 +161,25 @@ def tile_qdense_w_kernel(
 
         ctx.enter_context(tc.manual_schedule())
 
-        nc.vector.memset(wp[0][:].bitcast(I32), 0)
-        nc.vector.memset(brow[:], 0.0)
-        for q in range(1, NQ):
+        nc.vector.memset(brow[:].bitcast(I32), 0)
+        for q in range(NQ):
             nc.vector.memset(wp[q][:].bitcast(I32), 0)
         nc.vector.memset(sgn[:], 1.0)
         for q, t, h in NEGATIVE_BIAS:
             nc.vector.memset(sgn4[32 * q : 32 * q + 32, t, :, h], -1.0)
         make_identity(nc, ident[:])
 
-        nc.sync.dma_start(out=x_sb[:], in_=xv)
         for q in range(NQ):
-            nc.sync.dma_start(
+            nc.scalar.dma_start(
                 out=brow[32 * q : 32 * q + 1, :], in_=biases[q].rearrange("(o n) -> o n", o=1)
             )
-        for q in range(NQ):
-            load_scales(q)
+        nc.sync.dma_start(out=x_sb[:], in_=xv)
+        load_scales(0)
+        load_scales(2)
+        load_scales(3)
         for g in range(NG):
             load_words(0, g, 0, 2048)
+        load_scales(1)
         for q in (1, 2):
             for g in range(NG):
                 load_words(q, g, 0, 1024)

from contextlib import ExitStack

import concourse.mybir as mybir
from concourse.masks import make_identity

F32 = mybir.dt.float32
BF16 = mybir.dt.bfloat16
I32 = mybir.dt.int32
U32 = mybir.dt.uint32
U8 = mybir.dt.uint8
FP8X4 = mybir.dt.float8_e4m3fn_x4
ADD = mybir.AluOpType.add

FLOPS = 2 * 256 * 8192 * 2048

P = 128
NQ = 4
NG = 4
NT = 512
ALL_G = (0, 1, 2, 3)

VARIANTS = (
    ((1, 0, -1.0), (1, 1, 1.0)),
    ((0, 0, 1.0), (0, 1, -1.0)),
    ((0, 1, -1.0), (0, 0, 1.0)),
    ((1, 1, -1.0), (1, 0, 1.0)),
    ((1, 1, -1.0), (1, 0, -1.0)),
    ((0, 1, 1.0), (0, 0, 1.0)),
)
NEGATIVE_BIAS = ((1, 0, 0), (2, 0, 0), (3, 0, 0), (3, 0, 1), (2, 1, 0), (1, 1, 1))


def tile_qdense_w_kernel(
    tc,
    x,
    W_rr_words,
    W_rr_scales,
    W_ri_words,
    W_ri_scales,
    W_rj_words,
    W_rj_scales,
    W_rk_words,
    W_rk_scales,
    b_rr,
    b_ri,
    b_rj,
    b_rk,
    out,
):
    nc = tc.nc
    w_words = (W_rr_words, W_ri_words, W_rj_words, W_rk_words)
    w_scales = (W_rr_scales, W_ri_scales, W_rj_scales, W_rk_scales)
    biases = (b_rr, b_ri, b_rj, b_rk)

    with ExitStack() as ctx:
        keep = ctx.enter_context(tc.tile_pool(name="keep", bufs=1))
        psum = ctx.enter_context(tc.psum_pool(name="psum", bufs=1))

        ww = {}
        for q in range(NQ):
            for g in range(NG):
                ww[(q, g)] = keep.tile([P, 2048], U32, name="ww%d%d" % (q, g), align_bytes=64)
        wp = [keep.tile([P, 2048], U8, name="wp%d" % q, align_bytes=64) for q in range(NQ)]
        x_sb = keep.tile([P, 2, 2048], BF16, name="x_sb", align_bytes=64)
        grp = keep.tile([P, NG, 2, P, 4], BF16, name="grp", align_bytes=64)
        xwn = keep.tile([P, NG, 2, P], U32, name="xwn", align_bytes=64)
        xpn = keep.tile([P, NG, 2, P], U8, name="xpn", align_bytes=64)
        xwv = keep.tile([P, 6, NG, P], U32, name="xwv", align_bytes=64)
        xpv = keep.tile([P, 6, NG, P], U8, name="xpv", align_bytes=64)
        ident = keep.tile([P, P], F32, name="ident")
        brow = keep.tile([P, 2048], BF16, name="brow")
        sgn = keep.tile([P, 2, P], BF16, name="sgn")
        res = keep.tile([P, 4096], F32, name="res")

        out_v = out.rearrange("b (h f) -> (b h) f", h=2)
        xv = x.rearrange("b (h l f) -> (b h) l f", h=2, l=2)
        grp6 = grp[:].rearrange("p g l (b h) t -> p g l b h t", h=2)
        sgn4 = sgn[:].rearrange("p t (b h) -> p t b h", h=2)
        var = [
            keep.tile([P, NG, 64, 2, 4], BF16, name="var%d" % v, align_bytes=64) for v in range(6)
        ]

        def load_scales(q):
            for quad in range(4):
                dst = wp[q][32 * quad : 32 * quad + 16, :]
                src = w_scales[q][:, 4 * quad : 4 * quad + 4, :]
                if q < 2:
                    nc.sync.dma_start(out=dst.bitcast(I32), in_=src.bitcast(I32))
                else:
                    nc.gpsimd.dma_start(out=dst.bitcast(F32), in_=src.bitcast(F32))

        def load_words(q, g, c0, c1):
            src = w_words[q][g].rearrange("p n t -> p (n t)")[:, 4 * c0 : 4 * c1]
            nc.sync.dma_start(out=ww[(q, g)][:, c0:c1].bitcast(I32), in_=src.bitcast(I32))

        def halves(v, on_vector):
            for h in range(2):
                l, hs, sign = VARIANTS[v][h]
                dst = var[v][:, :, :, h, :]
                src = grp6[:, :, l, :, hs, :]
                if on_vector and sign > 0:
                    nc.vector.tensor_copy(out=dst, in_=src)
                elif on_vector:
                    nc.vector.tensor_scalar_mul(out=dst, in0=src, scalar1=-1.0)
                elif sign > 0:
                    nc.scalar.copy(out=dst, in_=src)
                else:
                    nc.scalar.mul(out=dst, in_=src, mul=-1.0)

        def quantise(v):
            nc.vector.quantize_mx(
                out=xwv[:, v, :, :].rearrange("p g m -> p (g m)").bitcast(FP8X4),
                scales=xpv[:, v, :, :].rearrange("p g m -> p (g m)"),
                in_=var[v][:].rearrange("p g b h t -> p (g b h t)"),
            )

        def mx_pass(acc, t, q, g, j):
            if q == 0:
                lw = xwn[:, g, t, :]
                lp = xpn[:, g, t, :]
            else:
                lw = xwv[:, 2 * (q - 1) + t, g, :]
                lp = xpv[:, 2 * (q - 1) + t, g, :]
            nc.tensor.matmul_mx(
                out=acc[:],
                lhsT=lw.bitcast(FP8X4),
                lhsT_scale=lp,
                rhs=ww[(q, g)][:, NT * j : NT * j + NT].bitcast(FP8X4),
                rhs_scale=wp[q][4 * g : P, NT * j : NT * j + NT],
                start=(q == 0 and g == 0),
                stop=(q == NQ - 1 and g == NG - 1),
            )

        def block(acc, q, js, gs):
            for g in gs:
                for t in range(2):
                    for j in js:
                        mx_pass(acc[(t, j)], t, q, g, j)

        def bias_round(js, bank0):
            made = []
            for t in range(2):
                for j in js:
                    bp = psum.tile([P, NT], F32, name="bp%d%d" % (t, j), tag="bank%d" % (bank0 + 2 * t + j % 2))
                    nc.tensor.matmul(
                        out=bp[:], lhsT=sgn[:, t, :], rhs=brow[:, NT * j : NT * j + NT], start=True, stop=True
                    )
                    made.append((bp, 2048 * t + NT * j))
            for i, (bp, c0) in enumerate(made):
                if i % 2 == 0:
                    nc.vector.tensor_copy(out=res[:, c0 : c0 + NT], in_=bp[:])
                else:
                    nc.scalar.copy(out=res[:, c0 : c0 + NT], in_=bp[:])

        def add_bias(acc, t, j):
            c0 = 2048 * t + NT * j
            nc.vector.tensor_tensor(out=res[:, c0 : c0 + NT], in0=acc[(t, j)][:], in1=res[:, c0 : c0 + NT], op=ADD)

        def store(c0, c1):
            nc.sync.dma_start(out=out_v[:, c0:c1], in_=res[:, c0:c1])

        ctx.enter_context(tc.manual_schedule())

        nc.vector.memset(brow[:].bitcast(I32), 0)
        for q in range(NQ):
            nc.vector.memset(wp[q][:].bitcast(I32), 0)
        nc.vector.memset(sgn[:], 1.0)
        for q, t, h in NEGATIVE_BIAS:
            nc.vector.memset(sgn4[32 * q : 32 * q + 32, t, :, h], -1.0)
        make_identity(nc, ident[:])

        for q in range(NQ):
            nc.scalar.dma_start(
                out=brow[32 * q : 32 * q + 1, :], in_=biases[q].rearrange("(o n) -> o n", o=1)
            )
        nc.sync.dma_start(out=x_sb[:], in_=xv)
        load_scales(0)
        load_scales(2)
        load_scales(3)
        for g in range(NG):
            load_words(0, g, 0, 2048)
        load_scales(1)
        for q in (1, 2):
            for g in range(NG):
                load_words(q, g, 0, 1024)
                load_words(q, g, 1024, 2048)
        for c0, c1 in ((0, 1024), (1024, 1536), (1536, 2048)):
            for g in range(NG):
                load_words(3, g, c0, c1)

        for g in range(NG):
            tps = psum.tile([P, 2, 2, P], F32, name="tps%d" % g, tag="bank%d" % (4 + g))
            for l in range(2):
                words = x_sb[:, l, :].bitcast(F32)
                w0 = 256 * g
                for u in range(2):
                    nc.tensor.transpose(tps[:, l, u, :], words[:, w0 + u : w0 + 256 : 2], ident[:])
            nc.scalar.copy(
                out=grp[:, g, :, :, :].bitcast(F32), in_=tps[:].rearrange("p l u m -> p l m u")
            )
            nc.vector.quantize_mx(
                out=xwn[:, g, :, :].rearrange("p l m -> p (l m)").bitcast(FP8X4),
                scales=xpn[:, g, :, :].rearrange("p l m -> p (l m)"),
                in_=grp[:, g, :, :, :].rearrange("p l m t -> p (l m t)"),
            )
        bias_round((0, 1), 0)
        bias_round((2, 3), 4)
        halves(0, True)
        halves(1, True)
        quantise(0)
        quantise(1)
        for v in (2, 3, 4, 5):
            halves(v, False)
            quantise(v)

        acc = {}
        for t in range(2):
            for j in range(4):
                acc[(t, j)] = psum.tile(
                    [P, NT], F32, name="acc%d%d" % (t, j), tag="bank%d" % (4 * (j // 2) + 2 * t + j % 2)
                )
        block(acc, 0, (0, 1, 2, 3), ALL_G)
        for q in (1, 2):
            for g in ALL_G:
                block(acc, q, (0, 1), (g,))
                block(acc, q, (2, 3), (g,))

        block(acc, 3, (0, 1), ALL_G)
        for t in range(2):
            for j in range(2):
                add_bias(acc, t, j)
        store(0, 1024)
        store(2048, 3072)
        for j in (2, 3):
            for t in range(2):
                for g in ALL_G:
                    mx_pass(acc[(t, j)], t, 3, g, j)
                if (t, j) == (1, 3):
                    for c in (0, NT // 2):
                        c0 = 2048 * t + NT * j + c
                        nc.vector.tensor_tensor(
                            out=res[:, c0 : c0 + NT // 2],
                            in0=acc[(t, j)][:, c : c + NT // 2],
                            in1=res[:, c0 : c0 + NT // 2],
                            op=ADD,
                        )
                        store(c0, c0 + NT // 2)
                else:
                    add_bias(acc, t, j)
                    store(2048 * t + NT * j, 2048 * t + NT * j + NT)
